import numpy as np
import ml_dtypes


def mxq(x, axis, fmt="e4m3"):
    dtype, down = {"e4m3": (ml_dtypes.float8_e4m3fn, 7), "e5m2": (ml_dtypes.float8_e5m2, 14)}[fmt]
    v = np.moveaxis(np.asarray(x, np.float32).astype(ml_dtypes.bfloat16).astype(np.float64), axis, -1)
    blocks = v.reshape(v.shape[:-1] + (-1, 32))
    amax = np.abs(blocks).max(-1, keepdims=True)
    byte = np.maximum(np.where(amax > 0, np.frexp(amax)[1] - 1 + 127, 0) - down, 1)
    scale = np.exp2(byte - 127.0)
    codes = (blocks / scale).astype(np.float32).astype(dtype).astype(np.float64)
    return np.moveaxis((codes * scale).reshape(v.shape), -1, axis)


WIDE = False


def mx_kscale(k):
    if not WIDE:
        return np.ones(k)
    levels = np.array([10, -10, 5, -5, 0])
    a = np.random.permutation(np.resize(levels, k // 512 * 4)).reshape(k // 512, 4)
    idx = np.arange(k)
    return np.exp2(a[idx // 512, idx % 128 // 32])


BF16 = ml_dtypes.bfloat16


def bf(x):
    return np.asarray(x, np.float32).astype(BF16)


def f64(x):
    return np.asarray(x).astype(np.float64)


B, N, O, M1, F, H, A = 128, 8, 128, 512, 1024, 256, 16
NG = 4
G = NG * H


def sigmoid(v):
    return 1.0 / (1.0 + np.exp(-v))


def setup_inputs():
    s, t = mx_kscale(M1), mx_kscale(F)
    r = np.random.standard_normal
    return {
        "f_hid": bf(np.maximum(r((B, N, M1)), 0.0) * s),
        "h0": bf(r((N, B, H))),
        "c0": bf(r((N, B, H))),
        "W2": bf(r((F, M1)) * 1.4 / np.sqrt(M1) / s[None, :] * t[:, None]),
        "b2": bf(r(F) * 0.2 * t),
        "W_ih": bf(r((N, G, F)) * 1.4 / np.sqrt(F) / t[None, None, :]),
        "W_hh": bf(r((N, G, H)) / np.sqrt(H)),
        "b_ih": bf(r((N, G)) * 0.2),
        "b_hh": bf(r((N, G)) * 0.2),
    }


def reference(f_hid, h0, c0, W2, b2, W_ih, W_hh, b_ih, b_hh):
    f = np.maximum((mxq(f64(f_hid), 2, "e4m3") @ mxq(f64(W2), 1, "e4m3").T) + f64(b2), 0.0)
    feats = f.transpose(1, 0, 2)
    gates = ((mxq(feats, 2, "e4m3") @ mxq(f64(W_ih), 2, "e4m3").transpose(0, 2, 1)) + f64(b_ih)[:, None, :]
             + f64(h0) @ f64(W_hh).transpose(0, 2, 1) + f64(b_hh)[:, None, :])
    i_g, f_g, g_g, o_g = np.split(gates, NG, axis=-1)
    i_g = sigmoid(i_g)
    f_g = sigmoid(f_g)
    g_g = np.tanh(g_g)
    o_g = sigmoid(o_g)
    c_new = f_g * f64(c0) + i_g * g_g
    h_new = o_g * np.tanh(c_new)
    return h_new, c_new

@@ -1,0 +1,233 @@
+import concourse.mybir as mybir
+from concourse.masks import make_identity
+
+F32 = mybir.dt.float32
+BF16 = mybir.dt.bfloat16
+U32 = mybir.dt.uint32
+U8 = mybir.dt.uint8
+FP8X4 = mybir.dt.float8_e4m3fn_x4
+FUNC = mybir.ActivationFunctionType
+ALU = mybir.AluOpType
+
+P = 128
+AGENTS = 8
+BATCH = 128
+M1 = 512
+F = 1024
+H = 256
+GATES = 4
+G = GATES * H
+BANK = 512
+K_PASS = 512
+PASS_WORDS = K_PASS // 2
+BLOCKS = 8
+
+FLOPS = 2 * BATCH * AGENTS * (M1 * F + F * G + H * G)
+
+
+def tile_ppo_actor_pa_kernel(tc, f_hid, h0, c0, W2, b2, W_ih, W_hh, b_ih, b_hh, out_0, out_1):
+    nc = tc.nc
+    with (
+        tc.tile_pool(name="keep", bufs=1) as keep,
+        tc.tile_pool(name="raw", bufs=3) as raw,
+        tc.tile_pool(name="stage", bufs=2) as stage,
+        tc.tile_pool(name="work", bufs=2) as work,
+        tc.psum_pool(name="flip", bufs=4) as flip,
+        tc.psum_pool(name="acc", bufs=4) as acc,
+    ):
+        identity = keep.tile([P, P], F32)
+        make_identity(nc, identity[:])
+
+        warm = keep.tile([P, 2], F32)
+        nc.vector.memset(warm[:], 0.0)
+        nc.scalar.activation(out=warm[:, 1:2], in_=warm[:, 0:1], func=FUNC.Sigmoid)
+
+        vec_rows = keep.tile([P, 2 * P], BF16)
+        nc.vector.memset(vec_rows[:].bitcast(F32), 0.0)
+        nc.sync.dma_start(out=vec_rows[0:32, :], in_=b_ih.rearrange("n (q w) -> (n q) w", w=2 * P))
+        nc.sync.dma_start(out=vec_rows[32:64, :], in_=b_hh.rearrange("n (q w) -> (n q) w", w=2 * P))
+        nc.sync.dma_start(out=vec_rows[64:68, :], in_=b2.rearrange("(r w) -> r w", w=2 * P))
+        fh_raw = keep.tile([P, AGENTS, M1], BF16)
+        nc.sync.dma_start(out=fh_raw[:], in_=f_hid)
+        w2_raw = keep.tile([P, 4, 2 * M1], BF16)
+        nc.sync.dma_start(out=w2_raw[:], in_=W2.rearrange("(r p e) k -> p r (e k)", p=P, e=2))
+        h0_raw = keep.tile([P, AGENTS, H], BF16)
+        nc.sync.dma_start(out=h0_raw[:], in_=h0.rearrange("n b k -> b n k"))
+        c0_sb = keep.tile([P, AGENTS, H], BF16)
+
+        def load_weights(n):
+            whh_raw = raw.tile([P, GATES, 2 * H], BF16, tag="whh_raw")
+            nc.sync.dma_start(out=whh_raw[:], in_=W_hh[n].rearrange("(q p j) k -> p q (j k)", p=P, j=2))
+            wih_raw = raw.tile([P, GATES, 2 * F], BF16, tag="wih_raw")
+            nc.sync.dma_start(out=wih_raw[:], in_=W_ih[n].rearrange("(q p j) k -> p q (j k)", p=P, j=2))
+            return whh_raw, wih_raw
+
+        def transpose_and_quantise(words, first_word, copy_out, codes, scales):
+            grouped = stage.tile([P, BLOCKS * P * 4], BF16, tag="grouped", align_bytes=64)
+            grouped_words = grouped[:].bitcast(F32)
+            for pair in range(BLOCKS // 2):
+                bank = flip.tile([P, BANK], F32, tag="flip")
+                for a in range(2):
+                    for u in range(2):
+                        nc.tensor.transpose(
+                            bank[:, (2 * a + u) * P : (2 * a + u + 1) * P],
+                            words[:, 2 * pair + a, first_word + u * P : first_word + (u + 1) * P],
+                            identity[:],
+                        )
+                copy_out(
+                    out=grouped_words[:, pair * BANK : (pair + 1) * BANK].rearrange("p (a c u) -> p a c u", a=2, u=2),
+                    in_=bank[:].rearrange("p (a u c) -> p a c u", a=2, u=2),
+                )
+            nc.vector.quantize_mx(out=codes.bitcast(FP8X4), scales=scales, in_=grouped[:])
+
+        vec_bank = flip.tile([P, BANK], F32, tag="flip")
+        nc.tensor.transpose(vec_bank[:, 0:P], vec_rows[:].bitcast(F32), identity[:])
+        vec_cols = keep.tile([P, 136], F32)
+        nc.vector.tensor_copy(out=vec_cols[:], in_=vec_bank[:].bitcast(BF16)[:, 0:136])
+        gate_bias = keep.tile([P, 64], F32)
+        nc.vector.tensor_tensor(out=gate_bias[:], in0=vec_cols[:, 0:64], in1=vec_cols[:, 64:128], op=ALU.add)
+        b2_cols = vec_cols[:, 128:136]
+
+        fh_codes = keep.tile([P, AGENTS * BATCH], U32, align_bytes=64)
+        fh_scales = keep.tile([P, AGENTS * BATCH], U8, align_bytes=64)
+        transpose_and_quantise(
+            fh_raw[:].rearrange("p n k -> p (n k)").bitcast(F32).rearrange("p (n w) -> p n w", n=AGENTS),
+            0, nc.scalar.copy, fh_codes[:], fh_scales[:],
+        )
+        w2_codes = keep.tile([P, F], U32, align_bytes=64)
+        w2_scales = keep.tile([P, F], U8, align_bytes=64)
+        transpose_and_quantise(
+            w2_raw[:].rearrange("p r k -> p (r k)").bitcast(F32).rearrange("p (s w) -> p s w", s=BLOCKS),
+            0, nc.vector.tensor_copy, w2_codes[:], w2_scales[:],
+        )
+
+        weights = {0: load_weights(0), 1: load_weights(1)}
+        nc.sync.dma_start(out=c0_sb[:], in_=c0.rearrange("n b k -> b n k"))
+
+        h0T = keep.tile([P, AGENTS * BATCH, 2], BF16)
+        h0_words = h0_raw[:].rearrange("p n k -> p (n k)").bitcast(F32)
+        for half in range(2):
+            bank = flip.tile([P, BANK], F32, tag="flip")
+            for i in range(4):
+                n = 4 * half + i
+                nc.tensor.transpose(bank[:, i * P : (i + 1) * P], h0_words[:, n * P : (n + 1) * P], identity[:])
+            nc.vector.tensor_copy(
+                out=h0T[:, half * BANK : (half + 1) * BANK, :].rearrange("p c e -> p (c e)"),
+                in_=bank[:].bitcast(BF16),
+            )
+
+        feat_codes = keep.tile([P, 2, AGENTS * BATCH], U32, align_bytes=64)
+        feat_scales = keep.tile([P, 2, AGENTS * BATCH], U8, align_bytes=64)
+        for c in range(2):
+            for cols in range(2):
+                planes = stage.tile([P, 4, BANK], BF16, tag="planes")
+                for t in range(4):
+                    s = 4 * c + t
+                    f_bank = acc.tile([P, BANK], F32, tag="acc")
+                    nc.tensor.matmul_mx(
+                        out=f_bank[:],
+                        lhsT=w2_codes[:, s * P : (s + 1) * P].bitcast(FP8X4),
+                        lhsT_scale=w2_scales[:, s * P : (s + 1) * P],
+                        rhs=fh_codes[:, cols * BANK : (cols + 1) * BANK].bitcast(FP8X4),
+                        rhs_scale=fh_scales[:, cols * BANK : (cols + 1) * BANK],
+                        start=True,
+                        stop=True,
+                    )
+                    nc.scalar.activation(out=planes[:, t, :], in_=f_bank[:], func=FUNC.Relu, bias=b2_cols[:, s : s + 1])
+                feat_grouped = stage.tile([P, BANK, 4], BF16, tag="feat_grouped", align_bytes=64)
+                nc.vector.tensor_copy(out=feat_grouped[:], in_=planes[:].rearrange("p t c -> p c t"))
+                nc.vector.quantize_mx(
+                    out=feat_codes[:, c, cols * BANK : (cols + 1) * BANK].bitcast(FP8X4),
+                    scales=feat_scales[:, c, cols * BANK : (cols + 1) * BANK],
+                    in_=feat_grouped[:].rearrange("p c t -> p (c t)"),
+                )
+
+        def prepare(n):
+            whh_raw, wih_raw = weights[n]
+            whhT = work.tile([P, G, 2], BF16, tag="whhT")
+            whh_words = whh_raw[:].rearrange("p q k -> p (q k)").bitcast(F32)
+            for half in range(2):
+                bank = flip.tile([P, BANK], F32, tag="flip")
+                for i in range(4):
+                    s = 4 * half + i
+                    nc.tensor.transpose(bank[:, i * P : (i + 1) * P], whh_words[:, s * P : (s + 1) * P], identity[:])
+                copy_out = nc.scalar.copy if half == 0 else nc.vector.tensor_copy
+                copy_out(
+                    out=whhT[:, half * BANK : (half + 1) * BANK, :].rearrange("p c e -> p (c e)"),
+                    in_=bank[:].bitcast(BF16),
+                )
+            wih_codes = work.tile([P, 2, G], U32, tag="wih_codes", align_bytes=64)
+            wih_scales = work.tile([P, 2, G], U8, tag="wih_scales", align_bytes=64)
+            wih_words = wih_raw[:].rearrange("p q k -> p (q k)").bitcast(F32).rearrange("p (s w) -> p s w", s=BLOCKS)
+            for c in range(2):
+                transpose_and_quantise(wih_words, c * PASS_WORDS, nc.scalar.copy, wih_codes[:, c, :], wih_scales[:, c, :])
+            return whhT, wih_codes, wih_scales
+
+        def cell(n, whhT, wih_codes, wih_scales):
+            gates = work.tile([P, G], F32, tag="gates")
+            for half in range(2):
+                cols = slice(half * BANK, (half + 1) * BANK)
+                hh_bank = acc.tile([P, BANK], F32, tag="acc")
+                for i in range(4):
+                    m = 8 * n + 4 * half + i
+                    nc.tensor.matmul(
+                        out=hh_bank[:, i * P : (i + 1) * P],
+                        lhsT=gate_bias[:, m : m + 1].to_broadcast([P, P]),
+                        rhs=identity[:],
+                        is_transpose=True,
+                        start=(i == 0),
+                        stop=False,
+                    )
+                for e in range(2):
+                    nc.tensor.matmul(
+                        out=hh_bank[:],
+                        lhsT=h0T[:, n * BATCH : (n + 1) * BATCH, e],
+                        rhs=whhT[:, cols, e],
+                        start=False,
+                        stop=(e == 1),
+                    )
+                hh_sb = work.tile([P, BANK], F32, tag="hh_sb")
+                nc.vector.tensor_copy(
+                    out=hh_sb[:].rearrange("b (q p j) -> b q p j", q=2, j=2),
+                    in_=hh_bank[:].rearrange("b (q j p) -> b q p j", q=2, j=2),
+                )
+                mx_bank = acc.tile([P, BANK], F32, tag="acc")
+                for c in range(2):
+                    nc.tensor.matmul_mx(
+                        out=mx_bank[:],
+                        lhsT=feat_codes[:, c, n * BATCH : (n + 1) * BATCH].bitcast(FP8X4),
+                        lhsT_scale=feat_scales[:, c, n * BATCH : (n + 1) * BATCH],
+                        rhs=wih_codes[:, c, cols].bitcast(FP8X4),
+                        rhs_scale=wih_scales[:, c, cols],
+                        start=(c == 0),
+                        stop=(c == 1),
+                    )
+                nc.vector.tensor_tensor(
+                    out=gates[:, cols].rearrange("b (q p j) -> b q p j", q=2, j=2),
+                    in0=mx_bank[:].rearrange("b (q j p) -> b q p j", q=2, j=2),
+                    in1=hh_sb[:].rearrange("b (q p j) -> b q p j", q=2, j=2),
+                    op=ALU.add,
+                )
+            squashed = work.tile([P, G], F32, tag="squashed")
+            nc.scalar.activation(out=squashed[:, 0 : 2 * H], in_=gates[:, 0 : 2 * H], func=FUNC.Sigmoid)
+            nc.scalar.activation(out=squashed[:, 2 * H : 3 * H], in_=gates[:, 2 * H : 3 * H], func=FUNC.Tanh)
+            nc.scalar.activation(out=squashed[:, 3 * H : 4 * H], in_=gates[:, 3 * H : 4 * H], func=FUNC.Sigmoid)
+            h_c = work.tile([P, 2, H], F32, tag="h_c")
+            kept = work.tile([P, H], F32, tag="kept")
+            nc.vector.tensor_tensor(out=kept[:], in0=squashed[:, H : 2 * H], in1=c0_sb[:, n, :], op=ALU.mult)
+            fresh = work.tile([P, H], F32, tag="fresh")
+            nc.vector.tensor_tensor(out=fresh[:], in0=squashed[:, 0:H], in1=squashed[:, 2 * H : 3 * H], op=ALU.mult)
+            nc.vector.tensor_tensor(out=h_c[:, 1, :], in0=kept[:], in1=fresh[:], op=ALU.add)
+            nc.sync.dma_start(out=out_1[n], in_=h_c[:, 1, :])
+            tanh_c = work.tile([P, H], F32, tag="tanh_c")
+            nc.scalar.activation(out=tanh_c[:], in_=h_c[:, 1, :], func=FUNC.Tanh)
+            nc.vector.tensor_tensor(out=h_c[:, 0, :], in0=squashed[:, 3 * H : 4 * H], in1=tanh_c[:], op=ALU.mult)
+            nc.sync.dma_start(out=out_0[n], in_=h_c[:, 0, :])
+
+        ready = prepare(0)
+        for n in range(AGENTS):
+            if n + 2 < AGENTS:
+                weights[n + 2] = load_weights(n + 2)
+            following = prepare(n + 1) if n + 1 < AGENTS else None
+            cell(n, *ready)
+            ready = following

@@ -15,12 +15,9 @@ BATCH = 128
 M1 = 512
 F = 1024
 H = 256
-GATES = 4
-G = GATES * H
+G = 4 * H
 BANK = 512
-K_PASS = 512
-PASS_WORDS = K_PASS // 2
-BLOCKS = 8
+PASS_WORDS = 256
 
 FLOPS = 2 * BATCH * AGENTS * (M1 * F + F * G + H * G)
 
@@ -29,11 +26,14 @@ def tile_ppo_actor_pa_kernel(tc, f_hid, h0, c0, W2, b2, W_ih, W_hh, b_ih, b_hh, 
     nc = tc.nc
     with (
         tc.tile_pool(name="keep", bufs=1) as keep,
-        tc.tile_pool(name="raw", bufs=3) as raw,
-        tc.tile_pool(name="stage", bufs=2) as stage,
+        tc.tile_pool(name="raw_hh", bufs=3) as raw_hh,
+        tc.tile_pool(name="raw_ih", bufs=6) as raw_ih,
+        tc.tile_pool(name="stage", bufs=3) as stage,
+        tc.tile_pool(name="units", bufs=8) as units,
         tc.tile_pool(name="work", bufs=2) as work,
         tc.psum_pool(name="flip", bufs=4) as flip,
         tc.psum_pool(name="acc", bufs=4) as acc,
+        tc.manual_schedule(),
     ):
         identity = keep.tile([P, P], F32)
         make_identity(nc, identity[:])
@@ -41,6 +41,19 @@ def tile_ppo_actor_pa_kernel(tc, f_hid, h0, c0, W2, b2, W_ih, W_hh, b_ih, b_hh, 
         warm = keep.tile([P, 2], F32)
         nc.vector.memset(warm[:], 0.0)
         nc.scalar.activation(out=warm[:, 1:2], in_=warm[:, 0:1], func=FUNC.Sigmoid)
+
+        whh_raw = {}
+        wih_raw = {}
+
+        def load_input_weights(n):
+            for half in range(2):
+                rows = W_ih[n, half * BANK : (half + 1) * BANK, :]
+                wih_raw[(n, half)] = raw_ih.tile([P, 2, 2 * F], BF16, name="wih_raw")
+                nc.sync.dma_start(out=wih_raw[(n, half)][:], in_=rows.rearrange("(q p j) k -> p q (j k)", p=P, j=2))
+
+        def load_recurrent_weights(n):
+            whh_raw[n] = raw_hh.tile([P, 4, 2 * H], BF16, name="whh_raw")
+            nc.sync.dma_start(out=whh_raw[n][:], in_=W_hh[n].rearrange("(q p j) k -> p q (j k)", p=P, j=2))
 
         vec_rows = keep.tile([P, 2 * P], BF16)
         nc.vector.memset(vec_rows[:].bitcast(F32), 0.0)
@@ -51,21 +64,21 @@ def tile_ppo_actor_pa_kernel(tc, f_hid, h0, c0, W2, b2, W_ih, W_hh, b_ih, b_hh, 
         nc.sync.dma_start(out=fh_raw[:], in_=f_hid)
         w2_raw = keep.tile([P, 4, 2 * M1], BF16)
         nc.sync.dma_start(out=w2_raw[:], in_=W2.rearrange("(r p e) k -> p r (e k)", p=P, e=2))
+        load_input_weights(0)
         h0_raw = keep.tile([P, AGENTS, H], BF16)
         nc.sync.dma_start(out=h0_raw[:], in_=h0.rearrange("n b k -> b n k"))
+        load_recurrent_weights(0)
+        load_recurrent_weights(1)
+        load_input_weights(1)
         c0_sb = keep.tile([P, AGENTS, H], BF16)
+        nc.sync.dma_start(out=c0_sb[:], in_=c0.rearrange("n b k -> b n k"))
+        load_recurrent_weights(2)
+        load_input_weights(2)
 
-        def load_weights(n):
-            whh_raw = raw.tile([P, GATES, 2 * H], BF16, tag="whh_raw")
-            nc.sync.dma_start(out=whh_raw[:], in_=W_hh[n].rearrange("(q p j) k -> p q (j k)", p=P, j=2))
-            wih_raw = raw.tile([P, GATES, 2 * F], BF16, tag="wih_raw")
-            nc.sync.dma_start(out=wih_raw[:], in_=W_ih[n].rearrange("(q p j) k -> p q (j k)", p=P, j=2))
-            return whh_raw, wih_raw
-
-        def transpose_and_quantise(words, first_word, copy_out, codes, scales):
-            grouped = stage.tile([P, BLOCKS * P * 4], BF16, tag="grouped", align_bytes=64)
+        def flip_unit(words, first_word, copy_out):
+            grouped = stage.tile([P, 4 * BANK], BF16, tag="grouped", align_bytes=64)
             grouped_words = grouped[:].bitcast(F32)
-            for pair in range(BLOCKS // 2):
+            for pair in range(2):
                 bank = flip.tile([P, BANK], F32, tag="flip")
                 for a in range(2):
                     for u in range(2):
@@ -78,7 +91,18 @@ def tile_ppo_actor_pa_kernel(tc, f_hid, h0, c0, W2, b2, W_ih, W_hh, b_ih, b_hh, 
                     out=grouped_words[:, pair * BANK : (pair + 1) * BANK].rearrange("p (a c u) -> p a c u", a=2, u=2),
                     in_=bank[:].rearrange("p (a u c) -> p a c u", a=2, u=2),
                 )
-            nc.vector.quantize_mx(out=codes.bitcast(FP8X4), scales=scales, in_=grouped[:])
+            return grouped
+
+        def flip_pairs(words, pairs, copy_outs):
+            for half in range(2):
+                bank = flip.tile([P, BANK], F32, tag="flip")
+                for i in range(4):
+                    s = 4 * half + i
+                    nc.tensor.transpose(bank[:, i * P : (i + 1) * P], words[:, s * P : (s + 1) * P], identity[:])
+                copy_outs[half](
+                    out=pairs[:, half * BANK : (half + 1) * BANK, :].rearrange("p c e -> p (c e)"),
+                    in_=bank[:].bitcast(BF16),
+                )
 
         vec_bank = flip.tile([P, BANK], F32, tag="flip")
         nc.tensor.transpose(vec_bank[:, 0:P], vec_rows[:].bitcast(F32), identity[:])
@@ -90,144 +114,181 @@ def tile_ppo_actor_pa_kernel(tc, f_hid, h0, c0, W2, b2, W_ih, W_hh, b_ih, b_hh, 
 
         fh_codes = keep.tile([P, AGENTS * BATCH], U32, align_bytes=64)
         fh_scales = keep.tile([P, AGENTS * BATCH], U8, align_bytes=64)
-        transpose_and_quantise(
-            fh_raw[:].rearrange("p n k -> p (n k)").bitcast(F32).rearrange("p (n w) -> p n w", n=AGENTS),
-            0, nc.scalar.copy, fh_codes[:], fh_scales[:],
-        )
         w2_codes = keep.tile([P, F], U32, align_bytes=64)
         w2_scales = keep.tile([P, F], U8, align_bytes=64)
-        transpose_and_quantise(
-            w2_raw[:].rearrange("p r k -> p (r k)").bitcast(F32).rearrange("p (s w) -> p s w", s=BLOCKS),
-            0, nc.vector.tensor_copy, w2_codes[:], w2_scales[:],
-        )
+        fh_words = fh_raw[:].rearrange("p n k -> p (n k)").bitcast(F32).rearrange("p (s w) -> p s w", s=8)
+        w2_words = w2_raw[:].rearrange("p r k -> p (r k)").bitcast(F32).rearrange("p (s w) -> p s w", s=8)
+        fh_grouped = [flip_unit(fh_words[:, 4 * i : 4 * i + 4, :], 0, nc.scalar.copy) for i in range(2)]
+        for i in range(2):
+            cols = slice(i * BANK, (i + 1) * BANK)
+            nc.vector.quantize_mx(out=fh_codes[:, cols].bitcast(FP8X4), scales=fh_scales[:, cols], in_=fh_grouped[i][:])
+        w2_grouped = [flip_unit(w2_words[:, 4 * i : 4 * i + 4, :], 0, nc.vector.tensor_copy) for i in range(2)]
+        for i in range(2):
+            cols = slice(i * BANK, (i + 1) * BANK)
+            nc.vector.quantize_mx(out=w2_codes[:, cols].bitcast(FP8X4), scales=w2_scales[:, cols], in_=w2_grouped[i][:])
 
-        weights = {0: load_weights(0), 1: load_weights(1)}
-        nc.sync.dma_start(out=c0_sb[:], in_=c0.rearrange("n b k -> b n k"))
+        wih_grouped = {}
+        wih_codes = {}
+        wih_scales = {}
+        whhT = {}
+        hh_sb = {}
+        gates = {}
+        squashed = {}
+        h_c = {}
 
-        h0T = keep.tile([P, AGENTS * BATCH, 2], BF16)
-        h0_words = h0_raw[:].rearrange("p n k -> p (n k)").bitcast(F32)
-        for half in range(2):
-            bank = flip.tile([P, BANK], F32, tag="flip")
-            for i in range(4):
-                n = 4 * half + i
-                nc.tensor.transpose(bank[:, i * P : (i + 1) * P], h0_words[:, n * P : (n + 1) * P], identity[:])
-            nc.vector.tensor_copy(
-                out=h0T[:, half * BANK : (half + 1) * BANK, :].rearrange("p c e -> p (c e)"),
-                in_=bank[:].bitcast(BF16),
+        def flip_input_weights(n, r):
+            if n == AGENTS:
+                return
+            half, c = divmod(r, 2)
+            words = wih_raw[(n, half)][:].rearrange("p q k -> p (q k)").bitcast(F32).rearrange("p (s w) -> p s w", s=4)
+            wih_grouped[(n, r)] = flip_unit(words, c * PASS_WORDS, nc.scalar.copy)
+
+        def quantise_input_weights(n, r):
+            if n == AGENTS:
+                return
+            wih_codes[(n, r)] = units.tile([P, BANK], U32, name="wih_codes", align_bytes=64)
+            wih_scales[(n, r)] = units.tile([P, BANK], U8, name="wih_scales", align_bytes=64)
+            nc.vector.quantize_mx(
+                out=wih_codes[(n, r)][:].bitcast(FP8X4), scales=wih_scales[(n, r)][:], in_=wih_grouped[(n, r)][:]
             )
+
+        def flip_recurrent_weights(n):
+            if n == AGENTS:
+                return
+            whhT[n] = work.tile([P, G, 2], BF16, name="whhT")
+            flip_pairs(
+                whh_raw[n][:].rearrange("p q k -> p (q k)").bitcast(F32), whhT[n], [nc.scalar.copy, nc.vector.tensor_copy]
+            )
+
+        def recurrent_group(n, half):
+            hh_bank = acc.tile([P, BANK], F32, tag="acc")
+            for i in range(4):
+                m = 8 * n + 4 * half + i
+                nc.tensor.matmul(
+                    out=hh_bank[:, i * P : (i + 1) * P],
+                    lhsT=gate_bias[:, m : m + 1].to_broadcast([P, P]),
+                    rhs=identity[:],
+                    is_transpose=True,
+                    start=(i == 0),
+                    stop=False,
+                )
+            for e in range(2):
+                nc.tensor.matmul(
+                    out=hh_bank[:],
+                    lhsT=h0T[:, n * BATCH : (n + 1) * BATCH, e],
+                    rhs=whhT[n][:, half * BANK : (half + 1) * BANK, e],
+                    start=False,
+                    stop=(e == 1),
+                )
+            hh_sb[(n, half)] = work.tile([P, BANK], F32, name="hh_sb")
+            nc.vector.tensor_copy(
+                out=hh_sb[(n, half)][:].rearrange("b (q p j) -> b q p j", q=2, j=2),
+                in_=hh_bank[:].rearrange("b (q j p) -> b q p j", q=2, j=2),
+            )
+
+        def input_group(n, half):
+            mx_bank = acc.tile([P, BANK], F32, tag="acc")
+            for c in range(2):
+                nc.tensor.matmul_mx(
+                    out=mx_bank[:],
+                    lhsT=feat_codes[:, c, n * BATCH : (n + 1) * BATCH].bitcast(FP8X4),
+                    lhsT_scale=feat_scales[:, c, n * BATCH : (n + 1) * BATCH],
+                    rhs=wih_codes[(n, 2 * half + c)][:].bitcast(FP8X4),
+                    rhs_scale=wih_scales[(n, 2 * half + c)][:],
+                    start=(c == 0),
+                    stop=(c == 1),
+                )
+            if half == 0:
+                gates[n] = work.tile([P, G], F32, name="gates")
+            nc.vector.tensor_tensor(
+                out=gates[n][:, half * BANK : (half + 1) * BANK].rearrange("b (q p j) -> b q p j", q=2, j=2),
+                in0=mx_bank[:].rearrange("b (q j p) -> b q p j", q=2, j=2),
+                in1=hh_sb[(n, half)][:].rearrange("b (q p j) -> b q p j", q=2, j=2),
+                op=ALU.add,
+            )
+
+        def squash_input_and_forget(n):
+            squashed[n] = work.tile([P, G], F32, name="squashed")
+            nc.scalar.activation(out=squashed[n][:, 0 : 2 * H], in_=gates[n][:, 0 : 2 * H], func=FUNC.Sigmoid)
+
+        def new_state(n):
+            nc.scalar.activation(out=squashed[n][:, 2 * H : 3 * H], in_=gates[n][:, 2 * H : 3 * H], func=FUNC.Tanh)
+            nc.scalar.activation(out=squashed[n][:, 3 * H : 4 * H], in_=gates[n][:, 3 * H : 4 * H], func=FUNC.Sigmoid)
+            h_c[n] = work.tile([P, 2, H], F32, name="h_c")
+            nc.vector.tensor_tensor(out=h_c[n][:, 0, :], in0=squashed[n][:, H : 2 * H], in1=c0_sb[:, n, :], op=ALU.mult)
+            fresh = work.tile([P, H], F32, tag="fresh")
+            nc.vector.tensor_tensor(out=fresh[:], in0=squashed[n][:, 0:H], in1=squashed[n][:, 2 * H : 3 * H], op=ALU.mult)
+            nc.vector.tensor_tensor(out=h_c[n][:, 1, :], in0=h_c[n][:, 0, :], in1=fresh[:], op=ALU.add)
+            nc.sync.dma_start(out=out_1[n], in_=h_c[n][:, 1, :])
+
+        def new_output(n):
+            if n < 0:
+                return
+            tanh_c = work.tile([P, H], F32, tag="tanh_c")
+            nc.scalar.activation(out=tanh_c[:], in_=h_c[n][:, 1, :], func=FUNC.Tanh)
+            nc.vector.tensor_tensor(out=h_c[n][:, 0, :], in0=squashed[n][:, 3 * H : 4 * H], in1=tanh_c[:], op=ALU.mult)
+            nc.sync.dma_start(out=out_0[n], in_=h_c[n][:, 0, :])
 
         feat_codes = keep.tile([P, 2, AGENTS * BATCH], U32, align_bytes=64)
         feat_scales = keep.tile([P, 2, AGENTS * BATCH], U8, align_bytes=64)
-        for c in range(2):
-            for cols in range(2):
-                planes = stage.tile([P, 4, BANK], BF16, tag="planes")
-                for t in range(4):
-                    s = 4 * c + t
-                    f_bank = acc.tile([P, BANK], F32, tag="acc")
-                    nc.tensor.matmul_mx(
-                        out=f_bank[:],
-                        lhsT=w2_codes[:, s * P : (s + 1) * P].bitcast(FP8X4),
-                        lhsT_scale=w2_scales[:, s * P : (s + 1) * P],
-                        rhs=fh_codes[:, cols * BANK : (cols + 1) * BANK].bitcast(FP8X4),
-                        rhs_scale=fh_scales[:, cols * BANK : (cols + 1) * BANK],
-                        start=True,
-                        stop=True,
-                    )
+        for r in range(4):
+            four_agents, c = divmod(r, 2)
+            cols = slice(four_agents * BANK, (four_agents + 1) * BANK)
+            planes = stage.tile([P, 4, BANK], BF16, tag="planes")
+            for t in range(4):
+                s = 4 * c + t
+                f_bank = acc.tile([P, BANK], F32, tag="acc")
+                nc.tensor.matmul_mx(
+                    out=f_bank[:],
+                    lhsT=w2_codes[:, s * P : (s + 1) * P].bitcast(FP8X4),
+                    lhsT_scale=w2_scales[:, s * P : (s + 1) * P],
+                    rhs=fh_codes[:, cols].bitcast(FP8X4),
+                    rhs_scale=fh_scales[:, cols],
+                    start=True,
+                    stop=True,
+                )
+                if t < 3:
                     nc.scalar.activation(out=planes[:, t, :], in_=f_bank[:], func=FUNC.Relu, bias=b2_cols[:, s : s + 1])
-                feat_grouped = stage.tile([P, BANK, 4], BF16, tag="feat_grouped", align_bytes=64)
-                nc.vector.tensor_copy(out=feat_grouped[:], in_=planes[:].rearrange("p t c -> p c t"))
-                nc.vector.quantize_mx(
-                    out=feat_codes[:, c, cols * BANK : (cols + 1) * BANK].bitcast(FP8X4),
-                    scales=feat_scales[:, c, cols * BANK : (cols + 1) * BANK],
-                    in_=feat_grouped[:].rearrange("p c t -> p (c t)"),
-                )
-
-        def prepare(n):
-            whh_raw, wih_raw = weights[n]
-            whhT = work.tile([P, G, 2], BF16, tag="whhT")
-            whh_words = whh_raw[:].rearrange("p q k -> p (q k)").bitcast(F32)
-            for half in range(2):
-                bank = flip.tile([P, BANK], F32, tag="flip")
-                for i in range(4):
-                    s = 4 * half + i
-                    nc.tensor.transpose(bank[:, i * P : (i + 1) * P], whh_words[:, s * P : (s + 1) * P], identity[:])
-                copy_out = nc.scalar.copy if half == 0 else nc.vector.tensor_copy
-                copy_out(
-                    out=whhT[:, half * BANK : (half + 1) * BANK, :].rearrange("p c e -> p (c e)"),
-                    in_=bank[:].bitcast(BF16),
-                )
-            wih_codes = work.tile([P, 2, G], U32, tag="wih_codes", align_bytes=64)
-            wih_scales = work.tile([P, 2, G], U8, tag="wih_scales", align_bytes=64)
-            wih_words = wih_raw[:].rearrange("p q k -> p (q k)").bitcast(F32).rearrange("p (s w) -> p s w", s=BLOCKS)
-            for c in range(2):
-                transpose_and_quantise(wih_words, c * PASS_WORDS, nc.scalar.copy, wih_codes[:, c, :], wih_scales[:, c, :])
-            return whhT, wih_codes, wih_scales
-
-        def cell(n, whhT, wih_codes, wih_scales):
-            gates = work.tile([P, G], F32, tag="gates")
-            for half in range(2):
-                cols = slice(half * BANK, (half + 1) * BANK)
-                hh_bank = acc.tile([P, BANK], F32, tag="acc")
-                for i in range(4):
-                    m = 8 * n + 4 * half + i
-                    nc.tensor.matmul(
-                        out=hh_bank[:, i * P : (i + 1) * P],
-                        lhsT=gate_bias[:, m : m + 1].to_broadcast([P, P]),
-                        rhs=identity[:],
-                        is_transpose=True,
-                        start=(i == 0),
-                        stop=False,
+                else:
+                    nc.vector.tensor_scalar(
+                        out=planes[:, t, :], in0=f_bank[:], scalar1=b2_cols[:, s : s + 1], scalar2=0.0,
+                        op0=ALU.add, op1=ALU.max,
                     )
-                for e in range(2):
-                    nc.tensor.matmul(
-                        out=hh_bank[:],
-                        lhsT=h0T[:, n * BATCH : (n + 1) * BATCH, e],
-                        rhs=whhT[:, cols, e],
-                        start=False,
-                        stop=(e == 1),
-                    )
-                hh_sb = work.tile([P, BANK], F32, tag="hh_sb")
-                nc.vector.tensor_copy(
-                    out=hh_sb[:].rearrange("b (q p j) -> b q p j", q=2, j=2),
-                    in_=hh_bank[:].rearrange("b (q j p) -> b q p j", q=2, j=2),
-                )
-                mx_bank = acc.tile([P, BANK], F32, tag="acc")
-                for c in range(2):
-                    nc.tensor.matmul_mx(
-                        out=mx_bank[:],
-                        lhsT=feat_codes[:, c, n * BATCH : (n + 1) * BATCH].bitcast(FP8X4),
-                        lhsT_scale=feat_scales[:, c, n * BATCH : (n + 1) * BATCH],
-                        rhs=wih_codes[:, c, cols].bitcast(FP8X4),
-                        rhs_scale=wih_scales[:, c, cols],
-                        start=(c == 0),
-                        stop=(c == 1),
-                    )
-                nc.vector.tensor_tensor(
-                    out=gates[:, cols].rearrange("b (q p j) -> b q p j", q=2, j=2),
-                    in0=mx_bank[:].rearrange("b (q j p) -> b q p j", q=2, j=2),
-                    in1=hh_sb[:].rearrange("b (q p j) -> b q p j", q=2, j=2),
-                    op=ALU.add,
-                )
-            squashed = work.tile([P, G], F32, tag="squashed")
-            nc.scalar.activation(out=squashed[:, 0 : 2 * H], in_=gates[:, 0 : 2 * H], func=FUNC.Sigmoid)
-            nc.scalar.activation(out=squashed[:, 2 * H : 3 * H], in_=gates[:, 2 * H : 3 * H], func=FUNC.Tanh)
-            nc.scalar.activation(out=squashed[:, 3 * H : 4 * H], in_=gates[:, 3 * H : 4 * H], func=FUNC.Sigmoid)
-            h_c = work.tile([P, 2, H], F32, tag="h_c")
-            kept = work.tile([P, H], F32, tag="kept")
-            nc.vector.tensor_tensor(out=kept[:], in0=squashed[:, H : 2 * H], in1=c0_sb[:, n, :], op=ALU.mult)
-            fresh = work.tile([P, H], F32, tag="fresh")
-            nc.vector.tensor_tensor(out=fresh[:], in0=squashed[:, 0:H], in1=squashed[:, 2 * H : 3 * H], op=ALU.mult)
-            nc.vector.tensor_tensor(out=h_c[:, 1, :], in0=kept[:], in1=fresh[:], op=ALU.add)
-            nc.sync.dma_start(out=out_1[n], in_=h_c[:, 1, :])
-            tanh_c = work.tile([P, H], F32, tag="tanh_c")
-            nc.scalar.activation(out=tanh_c[:], in_=h_c[:, 1, :], func=FUNC.Tanh)
-            nc.vector.tensor_tensor(out=h_c[:, 0, :], in0=squashed[:, 3 * H : 4 * H], in1=tanh_c[:], op=ALU.mult)
-            nc.sync.dma_start(out=out_0[n], in_=h_c[:, 0, :])
+            flip_input_weights(0, r)
+            feat_grouped = stage.tile([P, BANK, 4], BF16, tag="feat_grouped", align_bytes=64)
+            nc.vector.tensor_copy(
+                out=feat_grouped[:].rearrange("p (c i) t -> p c t i", i=4),
+                in_=planes[:].rearrange("p t (c i) -> p c t i", i=4),
+            )
+            nc.vector.quantize_mx(
+                out=feat_codes[:, c, cols].bitcast(FP8X4),
+                scales=feat_scales[:, c, cols],
+                in_=feat_grouped[:].rearrange("p c t -> p (c t)"),
+            )
+            quantise_input_weights(0, r)
 
-        ready = prepare(0)
+        h0T = keep.tile([P, AGENTS * BATCH, 2], BF16)
+        flip_pairs(h0_raw[:].rearrange("p n k -> p (n k)").bitcast(F32), h0T, [nc.scalar.copy, nc.vector.tensor_copy])
+        flip_recurrent_weights(0)
+
         for n in range(AGENTS):
-            if n + 2 < AGENTS:
-                weights[n + 2] = load_weights(n + 2)
-            following = prepare(n + 1) if n + 1 < AGENTS else None
-            cell(n, *ready)
-            ready = following
+            if n + 3 < AGENTS:
+                load_recurrent_weights(n + 3)
+                load_input_weights(n + 3)
+            flip_input_weights(n + 1, 0)
+            recurrent_group(n, 0)
+            new_output(n - 1)
+            quantise_input_weights(n + 1, 0)
+            flip_input_weights(n + 1, 1)
+            input_group(n, 0)
+            quantise_input_weights(n + 1, 1)
+            flip_input_weights(n + 1, 2)
+            squash_input_and_forget(n)
+            recurrent_group(n, 1)
+            quantise_input_weights(n + 1, 2)
+            flip_input_weights(n + 1, 3)
+            input_group(n, 1)
+            quantise_input_weights(n + 1, 3)
+            flip_recurrent_weights(n + 1)
+            new_state(n)
+        new_output(AGENTS - 1)

@@ -61,9 +61,12 @@ def tile_ppo_actor_pa_kernel(tc, f_hid, h0, c0, W2, b2, W_ih, W_hh, b_ih, b_hh, 
         nc.sync.dma_start(out=vec_rows[32:64, :], in_=b_hh.rearrange("n (q w) -> (n q) w", w=2 * P))
         nc.sync.dma_start(out=vec_rows[64:68, :], in_=b2.rearrange("(r w) -> r w", w=2 * P))
         fh_raw = keep.tile([P, AGENTS, M1], BF16)
-        nc.sync.dma_start(out=fh_raw[:], in_=f_hid)
         w2_raw = keep.tile([P, 4, 2 * M1], BF16)
-        nc.sync.dma_start(out=w2_raw[:], in_=W2.rearrange("(r p e) k -> p r (e k)", p=P, e=2))
+        w2_rows = W2.rearrange("(r p e) k -> p r (e k)", p=P, e=2)
+        for i in range(2):
+            nc.sync.dma_start(out=fh_raw[:, 4 * i : 4 * i + 4, :], in_=f_hid[:, 4 * i : 4 * i + 4, :])
+        for i in range(2):
+            nc.sync.dma_start(out=w2_raw[:, 2 * i : 2 * i + 2, :], in_=w2_rows[:, 2 * i : 2 * i + 2, :])
         load_input_weights(0)
         h0_raw = keep.tile([P, AGENTS, H], BF16)
         nc.sync.dma_start(out=h0_raw[:], in_=h0.rearrange("n b k -> b n k"))
@@ -93,13 +96,13 @@ def tile_ppo_actor_pa_kernel(tc, f_hid, h0, c0, W2, b2, W_ih, W_hh, b_ih, b_hh, 
                 )
             return grouped
 
-        def flip_pairs(words, pairs, copy_outs):
+        def flip_pairs(words, pairs, copy_out):
             for half in range(2):
                 bank = flip.tile([P, BANK], F32, tag="flip")
                 for i in range(4):
                     s = 4 * half + i
                     nc.tensor.transpose(bank[:, i * P : (i + 1) * P], words[:, s * P : (s + 1) * P], identity[:])
-                copy_outs[half](
+                copy_out(
                     out=pairs[:, half * BANK : (half + 1) * BANK, :].rearrange("p c e -> p (c e)"),
                     in_=bank[:].bitcast(BF16),
                 )
@@ -156,9 +159,7 @@ def tile_ppo_actor_pa_kernel(tc, f_hid, h0, c0, W2, b2, W_ih, W_hh, b_ih, b_hh, 
             if n == AGENTS:
                 return
             whhT[n] = work.tile([P, G, 2], BF16, name="whhT")
-            flip_pairs(
-                whh_raw[n][:].rearrange("p q k -> p (q k)").bitcast(F32), whhT[n], [nc.scalar.copy, nc.vector.tensor_copy]
-            )
+            flip_pairs(whh_raw[n][:].rearrange("p q k -> p (q k)").bitcast(F32), whhT[n], nc.vector.tensor_copy)
 
         def recurrent_group(n, half):
             hh_bank = acc.tile([P, BANK], F32, tag="acc")
@@ -209,16 +210,18 @@ def tile_ppo_actor_pa_kernel(tc, f_hid, h0, c0, W2, b2, W_ih, W_hh, b_ih, b_hh, 
 
         def squash_input_and_forget(n):
             squashed[n] = work.tile([P, G], F32, name="squashed")
+            h_c[n] = work.tile([P, 2, H], F32, name="h_c")
             nc.scalar.activation(out=squashed[n][:, 0 : 2 * H], in_=gates[n][:, 0 : 2 * H], func=FUNC.Sigmoid)
+            nc.gpsimd.tensor_tensor(out=h_c[n][:, 0, :], in0=squashed[n][:, H : 2 * H], in1=c0_sb[:, n, :], op=ALU.mult)
 
         def new_state(n):
+            if n < 0:
+                return
             nc.scalar.activation(out=squashed[n][:, 2 * H : 3 * H], in_=gates[n][:, 2 * H : 3 * H], func=FUNC.Tanh)
             nc.scalar.activation(out=squashed[n][:, 3 * H : 4 * H], in_=gates[n][:, 3 * H : 4 * H], func=FUNC.Sigmoid)
-            h_c[n] = work.tile([P, 2, H], F32, name="h_c")
-            nc.vector.tensor_tensor(out=h_c[n][:, 0, :], in0=squashed[n][:, H : 2 * H], in1=c0_sb[:, n, :], op=ALU.mult)
             fresh = work.tile([P, H], F32, tag="fresh")
-            nc.vector.tensor_tensor(out=fresh[:], in0=squashed[n][:, 0:H], in1=squashed[n][:, 2 * H : 3 * H], op=ALU.mult)
-            nc.vector.tensor_tensor(out=h_c[n][:, 1, :], in0=h_c[n][:, 0, :], in1=fresh[:], op=ALU.add)
+            nc.gpsimd.tensor_tensor(out=fresh[:], in0=squashed[n][:, 0:H], in1=squashed[n][:, 2 * H : 3 * H], op=ALU.mult)
+            nc.gpsimd.tensor_tensor(out=h_c[n][:, 1, :], in0=h_c[n][:, 0, :], in1=fresh[:], op=ALU.add)
             nc.sync.dma_start(out=out_1[n], in_=h_c[n][:, 1, :])
 
         def new_output(n):
@@ -226,7 +229,7 @@ def tile_ppo_actor_pa_kernel(tc, f_hid, h0, c0, W2, b2, W_ih, W_hh, b_ih, b_hh, 
                 return
             tanh_c = work.tile([P, H], F32, tag="tanh_c")
             nc.scalar.activation(out=tanh_c[:], in_=h_c[n][:, 1, :], func=FUNC.Tanh)
-            nc.vector.tensor_tensor(out=h_c[n][:, 0, :], in0=squashed[n][:, 3 * H : 4 * H], in1=tanh_c[:], op=ALU.mult)
+            nc.gpsimd.tensor_tensor(out=h_c[n][:, 0, :], in0=squashed[n][:, 3 * H : 4 * H], in1=tanh_c[:], op=ALU.mult)
             nc.sync.dma_start(out=out_0[n], in_=h_c[n][:, 0, :])
 
         feat_codes = keep.tile([P, 2, AGENTS * BATCH], U32, align_bytes=64)
@@ -268,7 +271,7 @@ def tile_ppo_actor_pa_kernel(tc, f_hid, h0, c0, W2, b2, W_ih, W_hh, b_ih, b_hh, 
             quantise_input_weights(0, r)
 
         h0T = keep.tile([P, AGENTS * BATCH, 2], BF16)
-        flip_pairs(h0_raw[:].rearrange("p n k -> p (n k)").bitcast(F32), h0T, [nc.scalar.copy, nc.vector.tensor_copy])
+        flip_pairs(h0_raw[:].rearrange("p n k -> p (n k)").bitcast(F32), h0T, nc.scalar.copy)
         flip_recurrent_weights(0)
 
         for n in range(AGENTS):
@@ -277,18 +280,19 @@ def tile_ppo_actor_pa_kernel(tc, f_hid, h0, c0, W2, b2, W_ih, W_hh, b_ih, b_hh, 
                 load_input_weights(n + 3)
             flip_input_weights(n + 1, 0)
             recurrent_group(n, 0)
-            new_output(n - 1)
             quantise_input_weights(n + 1, 0)
+            new_state(n - 1)
             flip_input_weights(n + 1, 1)
-            input_group(n, 0)
+            recurrent_group(n, 1)
             quantise_input_weights(n + 1, 1)
             flip_input_weights(n + 1, 2)
-            squash_input_and_forget(n)
-            recurrent_group(n, 1)
+            input_group(n, 0)
             quantise_input_weights(n + 1, 2)
+            new_output(n - 1)
             flip_input_weights(n + 1, 3)
             input_group(n, 1)
             quantise_input_weights(n + 1, 3)
+            squash_input_and_forget(n)
             flip_recurrent_weights(n + 1)
-            new_state(n)
+        new_state(AGENTS - 1)
         new_output(AGENTS - 1)

@@ -96,16 +96,15 @@ def tile_ppo_actor_pa_kernel(tc, f_hid, h0, c0, W2, b2, W_ih, W_hh, b_ih, b_hh, 
                 )
             return grouped
 
-        def flip_pairs(words, pairs, copy_out):
-            for half in range(2):
-                bank = flip.tile([P, BANK], F32, tag="flip")
-                for i in range(4):
-                    s = 4 * half + i
-                    nc.tensor.transpose(bank[:, i * P : (i + 1) * P], words[:, s * P : (s + 1) * P], identity[:])
-                copy_out(
-                    out=pairs[:, half * BANK : (half + 1) * BANK, :].rearrange("p c e -> p (c e)"),
-                    in_=bank[:].bitcast(BF16),
-                )
+        def flip_pairs(words, pairs, half, copy_out):
+            bank = flip.tile([P, BANK], F32, tag="flip")
+            for i in range(4):
+                s = 4 * half + i
+                nc.tensor.transpose(bank[:, i * P : (i + 1) * P], words[:, s * P : (s + 1) * P], identity[:])
+            copy_out(
+                out=pairs[:, half * BANK : (half + 1) * BANK, :].rearrange("p c e -> p (c e)"),
+                in_=bank[:].bitcast(BF16),
+            )
 
         vec_bank = flip.tile([P, BANK], F32, tag="flip")
         nc.tensor.transpose(vec_bank[:, 0:P], vec_rows[:].bitcast(F32), identity[:])
@@ -125,7 +124,7 @@ def tile_ppo_actor_pa_kernel(tc, f_hid, h0, c0, W2, b2, W_ih, W_hh, b_ih, b_hh, 
         for i in range(2):
             cols = slice(i * BANK, (i + 1) * BANK)
             nc.vector.quantize_mx(out=fh_codes[:, cols].bitcast(FP8X4), scales=fh_scales[:, cols], in_=fh_grouped[i][:])
-        w2_grouped = [flip_unit(w2_words[:, 4 * i : 4 * i + 4, :], 0, nc.vector.tensor_copy) for i in range(2)]
+        w2_grouped = [flip_unit(w2_words[:, 4 * i : 4 * i + 4, :], 0, nc.scalar.copy) for i in range(2)]
         for i in range(2):
             cols = slice(i * BANK, (i + 1) * BANK)
             nc.vector.quantize_mx(out=w2_codes[:, cols].bitcast(FP8X4), scales=w2_scales[:, cols], in_=w2_grouped[i][:])
@@ -134,7 +133,9 @@ def tile_ppo_actor_pa_kernel(tc, f_hid, h0, c0, W2, b2, W_ih, W_hh, b_ih, b_hh, 
         wih_codes = {}
         wih_scales = {}
         whhT = {}
+        hh_bank = {}
         hh_sb = {}
+        mx_bank = {}
         gates = {}
         squashed = {}
         h_c = {}
@@ -155,73 +156,86 @@ def tile_ppo_actor_pa_kernel(tc, f_hid, h0, c0, W2, b2, W_ih, W_hh, b_ih, b_hh, 
                 out=wih_codes[(n, r)][:].bitcast(FP8X4), scales=wih_scales[(n, r)][:], in_=wih_grouped[(n, r)][:]
             )
 
-        def flip_recurrent_weights(n):
+        def flip_recurrent_weights(n, half):
             if n == AGENTS:
                 return
-            whhT[n] = work.tile([P, G, 2], BF16, name="whhT")
-            flip_pairs(whh_raw[n][:].rearrange("p q k -> p (q k)").bitcast(F32), whhT[n], nc.vector.tensor_copy)
+            if half == 0:
+                whhT[n] = work.tile([P, G, 2], BF16, name="whhT")
+            copy_out = nc.scalar.copy if half == 0 else nc.vector.tensor_copy
+            flip_pairs(whh_raw[n][:].rearrange("p q k -> p (q k)").bitcast(F32), whhT[n], half, copy_out)
 
-        def recurrent_group(n, half):
-            hh_bank = acc.tile([P, BANK], F32, tag="acc")
+        def recurrent_matmul(n, half, e):
+            nc.tensor.matmul(
+                out=hh_bank[(n, half)][:],
+                lhsT=h0T[:, n * BATCH : (n + 1) * BATCH, e],
+                rhs=whhT[n][:, half * BANK : (half + 1) * BANK, e],
+                start=False,
+                stop=(e == 1),
+            )
+
+        def open_recurrent_group(n, half):
+            hh_bank[(n, half)] = acc.tile([P, BANK], F32, name="hh_bank", tag="acc")
             for i in range(4):
                 m = 8 * n + 4 * half + i
                 nc.tensor.matmul(
-                    out=hh_bank[:, i * P : (i + 1) * P],
+                    out=hh_bank[(n, half)][:, i * P : (i + 1) * P],
                     lhsT=gate_bias[:, m : m + 1].to_broadcast([P, P]),
                     rhs=identity[:],
                     is_transpose=True,
                     start=(i == 0),
                     stop=False,
                 )
-            for e in range(2):
-                nc.tensor.matmul(
-                    out=hh_bank[:],
-                    lhsT=h0T[:, n * BATCH : (n + 1) * BATCH, e],
-                    rhs=whhT[n][:, half * BANK : (half + 1) * BANK, e],
-                    start=False,
-                    stop=(e == 1),
-                )
+            recurrent_matmul(n, half, 0)
+
+        def close_recurrent_group(n, half):
+            recurrent_matmul(n, half, 1)
             hh_sb[(n, half)] = work.tile([P, BANK], F32, name="hh_sb")
             nc.vector.tensor_copy(
                 out=hh_sb[(n, half)][:].rearrange("b (q p j) -> b q p j", q=2, j=2),
-                in_=hh_bank[:].rearrange("b (q j p) -> b q p j", q=2, j=2),
+                in_=hh_bank[(n, half)][:].rearrange("b (q j p) -> b q p j", q=2, j=2),
             )
 
-        def input_group(n, half):
-            mx_bank = acc.tile([P, BANK], F32, tag="acc")
-            for c in range(2):
-                nc.tensor.matmul_mx(
-                    out=mx_bank[:],
-                    lhsT=feat_codes[:, c, n * BATCH : (n + 1) * BATCH].bitcast(FP8X4),
-                    lhsT_scale=feat_scales[:, c, n * BATCH : (n + 1) * BATCH],
-                    rhs=wih_codes[(n, 2 * half + c)][:].bitcast(FP8X4),
-                    rhs_scale=wih_scales[(n, 2 * half + c)][:],
-                    start=(c == 0),
-                    stop=(c == 1),
-                )
+        def input_pass(n, half, c):
+            if c == 0:
+                mx_bank[(n, half)] = acc.tile([P, BANK], F32, name="mx_bank", tag="acc")
+            nc.tensor.matmul_mx(
+                out=mx_bank[(n, half)][:],
+                lhsT=feat_codes[:, c, n * BATCH : (n + 1) * BATCH].bitcast(FP8X4),
+                lhsT_scale=feat_scales[:, c, n * BATCH : (n + 1) * BATCH],
+                rhs=wih_codes[(n, 2 * half + c)][:].bitcast(FP8X4),
+                rhs_scale=wih_scales[(n, 2 * half + c)][:],
+                start=(c == 0),
+                stop=(c == 1),
+            )
+            if c == 0:
+                return
             if half == 0:
                 gates[n] = work.tile([P, G], F32, name="gates")
             nc.vector.tensor_tensor(
                 out=gates[n][:, half * BANK : (half + 1) * BANK].rearrange("b (q p j) -> b q p j", q=2, j=2),
-                in0=mx_bank[:].rearrange("b (q j p) -> b q p j", q=2, j=2),
+                in0=mx_bank[(n, half)][:].rearrange("b (q j p) -> b q p j", q=2, j=2),
                 in1=hh_sb[(n, half)][:].rearrange("b (q p j) -> b q p j", q=2, j=2),
                 op=ALU.add,
             )
 
         def squash_input_and_forget(n):
             squashed[n] = work.tile([P, G], F32, name="squashed")
-            h_c[n] = work.tile([P, 2, H], F32, name="h_c")
             nc.scalar.activation(out=squashed[n][:, 0 : 2 * H], in_=gates[n][:, 0 : 2 * H], func=FUNC.Sigmoid)
-            nc.gpsimd.tensor_tensor(out=h_c[n][:, 0, :], in0=squashed[n][:, H : 2 * H], in1=c0_sb[:, n, :], op=ALU.mult)
 
-        def new_state(n):
+        def squash_cell_and_output(n):
             if n < 0:
                 return
             nc.scalar.activation(out=squashed[n][:, 2 * H : 3 * H], in_=gates[n][:, 2 * H : 3 * H], func=FUNC.Tanh)
             nc.scalar.activation(out=squashed[n][:, 3 * H : 4 * H], in_=gates[n][:, 3 * H : 4 * H], func=FUNC.Sigmoid)
+
+        def new_state(n):
+            if n < 0:
+                return
+            h_c[n] = work.tile([P, 2, H], F32, name="h_c")
+            nc.vector.tensor_tensor(out=h_c[n][:, 0, :], in0=squashed[n][:, H : 2 * H], in1=c0_sb[:, n, :], op=ALU.mult)
             fresh = work.tile([P, H], F32, tag="fresh")
-            nc.gpsimd.tensor_tensor(out=fresh[:], in0=squashed[n][:, 0:H], in1=squashed[n][:, 2 * H : 3 * H], op=ALU.mult)
-            nc.gpsimd.tensor_tensor(out=h_c[n][:, 1, :], in0=h_c[n][:, 0, :], in1=fresh[:], op=ALU.add)
+            nc.vector.tensor_tensor(out=fresh[:], in0=squashed[n][:, 0:H], in1=squashed[n][:, 2 * H : 3 * H], op=ALU.mult)
+            nc.vector.tensor_tensor(out=h_c[n][:, 1, :], in0=h_c[n][:, 0, :], in1=fresh[:], op=ALU.add)
             nc.sync.dma_start(out=out_1[n], in_=h_c[n][:, 1, :])
 
         def new_output(n):
@@ -229,7 +243,7 @@ def tile_ppo_actor_pa_kernel(tc, f_hid, h0, c0, W2, b2, W_ih, W_hh, b_ih, b_hh, 
                 return
             tanh_c = work.tile([P, H], F32, tag="tanh_c")
             nc.scalar.activation(out=tanh_c[:], in_=h_c[n][:, 1, :], func=FUNC.Tanh)
-            nc.gpsimd.tensor_tensor(out=h_c[n][:, 0, :], in0=squashed[n][:, 3 * H : 4 * H], in1=tanh_c[:], op=ALU.mult)
+            nc.vector.tensor_tensor(out=h_c[n][:, 0, :], in0=squashed[n][:, 3 * H : 4 * H], in1=tanh_c[:], op=ALU.mult)
             nc.sync.dma_start(out=out_0[n], in_=h_c[n][:, 0, :])
 
         feat_codes = keep.tile([P, 2, AGENTS * BATCH], U32, align_bytes=64)
@@ -271,28 +285,40 @@ def tile_ppo_actor_pa_kernel(tc, f_hid, h0, c0, W2, b2, W_ih, W_hh, b_ih, b_hh, 
             quantise_input_weights(0, r)
 
         h0T = keep.tile([P, AGENTS * BATCH, 2], BF16)
-        flip_pairs(h0_raw[:].rearrange("p n k -> p (n k)").bitcast(F32), h0T, nc.scalar.copy)
-        flip_recurrent_weights(0)
+        for half in range(2):
+            flip_pairs(h0_raw[:].rearrange("p n k -> p (n k)").bitcast(F32), h0T, half, nc.scalar.copy)
+        for half in range(2):
+            flip_recurrent_weights(0, half)
 
         for n in range(AGENTS):
             if n + 3 < AGENTS:
                 load_recurrent_weights(n + 3)
                 load_input_weights(n + 3)
             flip_input_weights(n + 1, 0)
-            recurrent_group(n, 0)
+            squash_cell_and_output(n - 1)
+            open_recurrent_group(n, 0)
+            input_pass(n, 0, 0)
             quantise_input_weights(n + 1, 0)
             new_state(n - 1)
+
             flip_input_weights(n + 1, 1)
-            recurrent_group(n, 1)
+            flip_recurrent_weights(n + 1, 0)
+            close_recurrent_group(n, 0)
+            input_pass(n, 0, 1)
             quantise_input_weights(n + 1, 1)
+
             flip_input_weights(n + 1, 2)
-            input_group(n, 0)
-            quantise_input_weights(n + 1, 2)
             new_output(n - 1)
+            open_recurrent_group(n, 1)
+            input_pass(n, 1, 0)
+            quantise_input_weights(n + 1, 2)
+
             flip_input_weights(n + 1, 3)
-            input_group(n, 1)
-            quantise_input_weights(n + 1, 3)
             squash_input_and_forget(n)
-            flip_recurrent_weights(n + 1)
+            flip_recurrent_weights(n + 1, 1)
+            close_recurrent_group(n, 1)
+            input_pass(n, 1, 1)
+            quantise_input_weights(n + 1, 3)
+        squash_cell_and_output(AGENTS - 1)
         new_state(AGENTS - 1)
         new_output(AGENTS - 1)

import concourse.mybir as mybir
from concourse.masks import make_identity

F32 = mybir.dt.float32
BF16 = mybir.dt.bfloat16
U32 = mybir.dt.uint32
U8 = mybir.dt.uint8
FP8X4 = mybir.dt.float8_e4m3fn_x4
FUNC = mybir.ActivationFunctionType
ALU = mybir.AluOpType

P = 128
AGENTS = 8
BATCH = 128
M1 = 512
F = 1024
H = 256
G = 4 * H
BANK = 512
PASS_WORDS = 256

FLOPS = 2 * BATCH * AGENTS * (M1 * F + F * G + H * G)


def tile_ppo_actor_pa_kernel(tc, f_hid, h0, c0, W2, b2, W_ih, W_hh, b_ih, b_hh, out_0, out_1):
    nc = tc.nc
    with (
        tc.tile_pool(name="keep", bufs=1) as keep,
        tc.tile_pool(name="raw_hh", bufs=3) as raw_hh,
        tc.tile_pool(name="raw_ih", bufs=6) as raw_ih,
        tc.tile_pool(name="stage", bufs=3) as stage,
        tc.tile_pool(name="units", bufs=8) as units,
        tc.tile_pool(name="work", bufs=2) as work,
        tc.psum_pool(name="flip", bufs=4) as flip,
        tc.psum_pool(name="acc", bufs=4) as acc,
        tc.manual_schedule(),
    ):
        identity = keep.tile([P, P], F32)
        make_identity(nc, identity[:])

        warm = keep.tile([P, 2], F32)
        nc.vector.memset(warm[:], 0.0)
        nc.scalar.activation(out=warm[:, 1:2], in_=warm[:, 0:1], func=FUNC.Sigmoid)

        whh_raw = {}
        wih_raw = {}

        def load_input_weights(n):
            for half in range(2):
                rows = W_ih[n, half * BANK : (half + 1) * BANK, :]
                wih_raw[(n, half)] = raw_ih.tile([P, 2, 2 * F], BF16, name="wih_raw")
                nc.sync.dma_start(out=wih_raw[(n, half)][:], in_=rows.rearrange("(q p j) k -> p q (j k)", p=P, j=2))

        def load_recurrent_weights(n):
            whh_raw[n] = raw_hh.tile([P, 4, 2 * H], BF16, name="whh_raw")
            nc.sync.dma_start(out=whh_raw[n][:], in_=W_hh[n].rearrange("(q p j) k -> p q (j k)", p=P, j=2))

        vec_rows = keep.tile([P, 2 * P], BF16)
        nc.vector.memset(vec_rows[:].bitcast(F32), 0.0)
        nc.sync.dma_start(out=vec_rows[0:32, :], in_=b_ih.rearrange("n (q w) -> (n q) w", w=2 * P))
        nc.sync.dma_start(out=vec_rows[32:64, :], in_=b_hh.rearrange("n (q w) -> (n q) w", w=2 * P))
        nc.sync.dma_start(out=vec_rows[64:68, :], in_=b2.rearrange("(r w) -> r w", w=2 * P))
        fh_raw = keep.tile([P, AGENTS, M1], BF16)
        w2_raw = keep.tile([P, 4, 2 * M1], BF16)
        w2_rows = W2.rearrange("(r p e) k -> p r (e k)", p=P, e=2)
        for i in range(2):
            nc.sync.dma_start(out=fh_raw[:, 4 * i : 4 * i + 4, :], in_=f_hid[:, 4 * i : 4 * i + 4, :])
        for i in range(2):
            nc.sync.dma_start(out=w2_raw[:, 2 * i : 2 * i + 2, :], in_=w2_rows[:, 2 * i : 2 * i + 2, :])
        load_input_weights(0)
        h0_raw = keep.tile([P, AGENTS, H], BF16)
        nc.sync.dma_start(out=h0_raw[:], in_=h0.rearrange("n b k -> b n k"))
        load_recurrent_weights(0)
        load_recurrent_weights(1)
        load_input_weights(1)
        c0_sb = keep.tile([P, AGENTS, H], BF16)
        nc.sync.dma_start(out=c0_sb[:], in_=c0.rearrange("n b k -> b n k"))
        load_recurrent_weights(2)
        load_input_weights(2)

        def flip_unit(words, first_word, copy_out):
            grouped = stage.tile([P, 4 * BANK], BF16, tag="grouped", align_bytes=64)
            grouped_words = grouped[:].bitcast(F32)
            for pair in range(2):
                bank = flip.tile([P, BANK], F32, tag="flip")
                for a in range(2):
                    for u in range(2):
                        nc.tensor.transpose(
                            bank[:, (2 * a + u) * P : (2 * a + u + 1) * P],
                            words[:, 2 * pair + a, first_word + u * P : first_word + (u + 1) * P],
                            identity[:],
                        )
                copy_out(
                    out=grouped_words[:, pair * BANK : (pair + 1) * BANK].rearrange("p (a c u) -> p a c u", a=2, u=2),
                    in_=bank[:].rearrange("p (a u c) -> p a c u", a=2, u=2),
                )
            return grouped

        def flip_pairs(words, pairs, half, copy_out):
            bank = flip.tile([P, BANK], F32, tag="flip")
            for i in range(4):
                s = 4 * half + i
                nc.tensor.transpose(bank[:, i * P : (i + 1) * P], words[:, s * P : (s + 1) * P], identity[:])
            copy_out(
                out=pairs[:, half * BANK : (half + 1) * BANK, :].rearrange("p c e -> p (c e)"),
                in_=bank[:].bitcast(BF16),
            )

        vec_bank = flip.tile([P, BANK], F32, tag="flip")
        nc.tensor.transpose(vec_bank[:, 0:P], vec_rows[:].bitcast(F32), identity[:])
        vec_cols = keep.tile([P, 136], F32)
        nc.vector.tensor_copy(out=vec_cols[:], in_=vec_bank[:].bitcast(BF16)[:, 0:136])
        gate_bias = keep.tile([P, 64], F32)
        nc.vector.tensor_tensor(out=gate_bias[:], in0=vec_cols[:, 0:64], in1=vec_cols[:, 64:128], op=ALU.add)
        b2_cols = vec_cols[:, 128:136]

        fh_codes = keep.tile([P, AGENTS * BATCH], U32, align_bytes=64)
        fh_scales = keep.tile([P, AGENTS * BATCH], U8, align_bytes=64)
        w2_codes = keep.tile([P, F], U32, align_bytes=64)
        w2_scales = keep.tile([P, F], U8, align_bytes=64)
        fh_words = fh_raw[:].rearrange("p n k -> p (n k)").bitcast(F32).rearrange("p (s w) -> p s w", s=8)
        w2_words = w2_raw[:].rearrange("p r k -> p (r k)").bitcast(F32).rearrange("p (s w) -> p s w", s=8)
        fh_grouped = [flip_unit(fh_words[:, 4 * i : 4 * i + 4, :], 0, nc.scalar.copy) for i in range(2)]
        for i in range(2):
            cols = slice(i * BANK, (i + 1) * BANK)
            nc.vector.quantize_mx(out=fh_codes[:, cols].bitcast(FP8X4), scales=fh_scales[:, cols], in_=fh_grouped[i][:])
        w2_grouped = [flip_unit(w2_words[:, 4 * i : 4 * i + 4, :], 0, nc.scalar.copy) for i in range(2)]
        for i in range(2):
            cols = slice(i * BANK, (i + 1) * BANK)
            nc.vector.quantize_mx(out=w2_codes[:, cols].bitcast(FP8X4), scales=w2_scales[:, cols], in_=w2_grouped[i][:])

        wih_grouped = {}
        wih_codes = {}
        wih_scales = {}
        whhT = {}
        hh_bank = {}
        hh_sb = {}
        mx_bank = {}
        gates = {}
        squashed = {}
        h_c = {}

        def flip_input_weights(n, r):
            if n == AGENTS:
                return
            half, c = divmod(r, 2)
            words = wih_raw[(n, half)][:].rearrange("p q k -> p (q k)").bitcast(F32).rearrange("p (s w) -> p s w", s=4)
            wih_grouped[(n, r)] = flip_unit(words, c * PASS_WORDS, nc.scalar.copy)

        def quantise_input_weights(n, r):
            if n == AGENTS:
                return
            wih_codes[(n, r)] = units.tile([P, BANK], U32, name="wih_codes", align_bytes=64)
            wih_scales[(n, r)] = units.tile([P, BANK], U8, name="wih_scales", align_bytes=64)
            nc.vector.quantize_mx(
                out=wih_codes[(n, r)][:].bitcast(FP8X4), scales=wih_scales[(n, r)][:], in_=wih_grouped[(n, r)][:]
            )

        def flip_recurrent_weights(n, half):
            if n == AGENTS:
                return
            if half == 0:
                whhT[n] = work.tile([P, G, 2], BF16, name="whhT")
            copy_out = nc.scalar.copy if half == 0 else nc.vector.tensor_copy
            flip_pairs(whh_raw[n][:].rearrange("p q k -> p (q k)").bitcast(F32), whhT[n], half, copy_out)

        def recurrent_matmul(n, half, e):
            nc.tensor.matmul(
                out=hh_bank[(n, half)][:],
                lhsT=h0T[:, n * BATCH : (n + 1) * BATCH, e],
                rhs=whhT[n][:, half * BANK : (half + 1) * BANK, e],
                start=False,
                stop=(e == 1),
            )

        def open_recurrent_group(n, half):
            hh_bank[(n, half)] = acc.tile([P, BANK], F32, name="hh_bank", tag="acc")
            for i in range(4):
                m = 8 * n + 4 * half + i
                nc.tensor.matmul(
                    out=hh_bank[(n, half)][:, i * P : (i + 1) * P],
                    lhsT=gate_bias[:, m : m + 1].to_broadcast([P, P]),
                    rhs=identity[:],
                    is_transpose=True,
                    start=(i == 0),
                    stop=False,
                )
            recurrent_matmul(n, half, 0)

        def close_recurrent_group(n, half):
            recurrent_matmul(n, half, 1)
            hh_sb[(n, half)] = work.tile([P, BANK], F32, name="hh_sb")
            nc.vector.tensor_copy(
                out=hh_sb[(n, half)][:].rearrange("b (q p j) -> b q p j", q=2, j=2),
                in_=hh_bank[(n, half)][:].rearrange("b (q j p) -> b q p j", q=2, j=2),
            )

        def input_pass(n, half, c):
            if c == 0:
                mx_bank[(n, half)] = acc.tile([P, BANK], F32, name="mx_bank", tag="acc")
            nc.tensor.matmul_mx(
                out=mx_bank[(n, half)][:],
                lhsT=feat_codes[:, c, n * BATCH : (n + 1) * BATCH].bitcast(FP8X4),
                lhsT_scale=feat_scales[:, c, n * BATCH : (n + 1) * BATCH],
                rhs=wih_codes[(n, 2 * half + c)][:].bitcast(FP8X4),
                rhs_scale=wih_scales[(n, 2 * half + c)][:],
                start=(c == 0),
                stop=(c == 1),
            )
            if c == 0:
                return
            if half == 0:
                gates[n] = work.tile([P, G], F32, name="gates")
            nc.vector.tensor_tensor(
                out=gates[n][:, half * BANK : (half + 1) * BANK].rearrange("b (q p j) -> b q p j", q=2, j=2),
                in0=mx_bank[(n, half)][:].rearrange("b (q j p) -> b q p j", q=2, j=2),
                in1=hh_sb[(n, half)][:].rearrange("b (q p j) -> b q p j", q=2, j=2),
                op=ALU.add,
            )

        def squash_input_and_forget(n):
            squashed[n] = work.tile([P, G], F32, name="squashed")
            nc.scalar.activation(out=squashed[n][:, 0 : 2 * H], in_=gates[n][:, 0 : 2 * H], func=FUNC.Sigmoid)

        def squash_cell_and_output(n):
            if n < 0:
                return
            nc.scalar.activation(out=squashed[n][:, 2 * H : 3 * H], in_=gates[n][:, 2 * H : 3 * H], func=FUNC.Tanh)
            nc.scalar.activation(out=squashed[n][:, 3 * H : 4 * H], in_=gates[n][:, 3 * H : 4 * H], func=FUNC.Sigmoid)

        def new_state(n):
            if n < 0:
                return
            h_c[n] = work.tile([P, 2, H], F32, name="h_c")
            nc.vector.tensor_tensor(out=h_c[n][:, 0, :], in0=squashed[n][:, H : 2 * H], in1=c0_sb[:, n, :], op=ALU.mult)
            fresh = work.tile([P, H], F32, tag="fresh")
            nc.vector.tensor_tensor(out=fresh[:], in0=squashed[n][:, 0:H], in1=squashed[n][:, 2 * H : 3 * H], op=ALU.mult)
            nc.vector.tensor_tensor(out=h_c[n][:, 1, :], in0=h_c[n][:, 0, :], in1=fresh[:], op=ALU.add)
            nc.sync.dma_start(out=out_1[n], in_=h_c[n][:, 1, :])

        def new_output(n):
            if n < 0:
                return
            tanh_c = work.tile([P, H], F32, tag="tanh_c")
            nc.scalar.activation(out=tanh_c[:], in_=h_c[n][:, 1, :], func=FUNC.Tanh)
            nc.vector.tensor_tensor(out=h_c[n][:, 0, :], in0=squashed[n][:, 3 * H : 4 * H], in1=tanh_c[:], op=ALU.mult)
            nc.sync.dma_start(out=out_0[n], in_=h_c[n][:, 0, :])

        feat_codes = keep.tile([P, 2, AGENTS * BATCH], U32, align_bytes=64)
        feat_scales = keep.tile([P, 2, AGENTS * BATCH], U8, align_bytes=64)
        for r in range(4):
            four_agents, c = divmod(r, 2)
            cols = slice(four_agents * BANK, (four_agents + 1) * BANK)
            planes = stage.tile([P, 4, BANK], BF16, tag="planes")
            for t in range(4):
                s = 4 * c + t
                f_bank = acc.tile([P, BANK], F32, tag="acc")
                nc.tensor.matmul_mx(
                    out=f_bank[:],
                    lhsT=w2_codes[:, s * P : (s + 1) * P].bitcast(FP8X4),
                    lhsT_scale=w2_scales[:, s * P : (s + 1) * P],
                    rhs=fh_codes[:, cols].bitcast(FP8X4),
                    rhs_scale=fh_scales[:, cols],
                    start=True,
                    stop=True,
                )
                if t < 3:
                    nc.scalar.activation(out=planes[:, t, :], in_=f_bank[:], func=FUNC.Relu, bias=b2_cols[:, s : s + 1])
                else:
                    nc.vector.tensor_scalar(
                        out=planes[:, t, :], in0=f_bank[:], scalar1=b2_cols[:, s : s + 1], scalar2=0.0,
                        op0=ALU.add, op1=ALU.max,
                    )
            flip_input_weights(0, r)
            feat_grouped = stage.tile([P, BANK, 4], BF16, tag="feat_grouped", align_bytes=64)
            nc.vector.tensor_copy(
                out=feat_grouped[:].rearrange("p (c i) t -> p c t i", i=4),
                in_=planes[:].rearrange("p t (c i) -> p c t i", i=4),
            )
            nc.vector.quantize_mx(
                out=feat_codes[:, c, cols].bitcast(FP8X4),
                scales=feat_scales[:, c, cols],
                in_=feat_grouped[:].rearrange("p c t -> p (c t)"),
            )
            quantise_input_weights(0, r)

        h0T = keep.tile([P, AGENTS * BATCH, 2], BF16)
        for half in range(2):
            flip_pairs(h0_raw[:].rearrange("p n k -> p (n k)").bitcast(F32), h0T, half, nc.scalar.copy)
        for half in range(2):
            flip_recurrent_weights(0, half)

        for n in range(AGENTS):
            if n + 3 < AGENTS:
                load_recurrent_weights(n + 3)
                load_input_weights(n + 3)
            flip_input_weights(n + 1, 0)
            squash_cell_and_output(n - 1)
            open_recurrent_group(n, 0)
            input_pass(n, 0, 0)
            quantise_input_weights(n + 1, 0)
            new_state(n - 1)

            flip_input_weights(n + 1, 1)
            flip_recurrent_weights(n + 1, 0)
            close_recurrent_group(n, 0)
            input_pass(n, 0, 1)
            quantise_input_weights(n + 1, 1)

            flip_input_weights(n + 1, 2)
            new_output(n - 1)
            open_recurrent_group(n, 1)
            input_pass(n, 1, 0)
            quantise_input_weights(n + 1, 2)

            flip_input_weights(n + 1, 3)
            squash_input_and_forget(n)
            flip_recurrent_weights(n + 1, 1)
            close_recurrent_group(n, 1)
            input_pass(n, 1, 1)
            quantise_input_weights(n + 1, 3)
        squash_cell_and_output(AGENTS - 1)
        new_state(AGENTS - 1)
        new_output(AGENTS - 1)
